import numpy as np
import ml_dtypes

BF16 = ml_dtypes.bfloat16


def bf(x):
    return np.asarray(x, np.float32).astype(BF16)


def f32(x):
    return np.asarray(x, np.float32)


def f64(x):
    return np.asarray(x).astype(np.float64)


def striped(idx):
    return np.tile(idx.reshape(-1, 16).T, (8, 1))


B, L, D, M, S, N = 4, 32, 128, 256, 256, 128


def setup_inputs():
    return {"table": bf(np.random.standard_normal((D, S))), "w": bf(np.random.standard_normal((D, M)) / np.sqrt(D)), "b": f32(0.1 * np.random.standard_normal((M, 1))), "offs": striped(np.random.permutation(np.tile(np.arange(S), 2))[:N])}


def reference(table, w, b, offs):
    idx = offs[:16].T.reshape(-1)
    kv = f64(w).T @ f64(table)[:, idx] + f64(b)
    relay = kv.reshape(M, B, L).sum(axis=2) * (1.0 / L)
    return np.concatenate([kv, relay], axis=1)

@@ -1,0 +1,54 @@
+import concourse.mybir as mybir
+
+BF16, F32, U16 = mybir.dt.bfloat16, mybir.dt.float32, mybir.dt.uint16
+
+P = 128
+CHARS = 256
+N = 128
+SENTENCES, LENGTH = 4, 32
+BLOCKS = 2
+
+FLOPS = 2 * P * BLOCKS * P * N
+BYTES = P * N * 2 + P * BLOCKS * P * 2 + BLOCKS * P * 4 + P * (N // 16) * 2 + BLOCKS * P * (N + SENTENCES) * 4
+
+
+def tile_ner_kernel(tc, table, w, b, offs, out):
+    nc = tc.nc
+    with (
+        tc.tile_pool(name="held", bufs=1) as held,
+        tc.tile_pool(name="rows", bufs=BLOCKS) as rows,
+        tc.psum_pool(name="psum", bufs=BLOCKS) as psum,
+    ):
+        offsets = held.tile([P, N // 16], U16, name="offsets")
+        nc.sync.dma_start(offsets[:], offs)
+        window = held.tile([P, CHARS], BF16, name="window")
+        nc.sync.dma_start(window[:], table)
+        weights = held.tile([P, BLOCKS * P], BF16, name="weights")
+        nc.scalar.dma_start(weights[:], w)
+        biases = []
+        for block in range(BLOCKS):
+            bias = held.tile([P, 1], F32, name=f"bias{block}")
+            nc.scalar.dma_start(bias[:], b[block * P : (block + 1) * P, :])
+            biases.append(bias)
+
+        for block in range(BLOCKS):
+            product = psum.tile([P, N], F32, name="product")
+            nc.tensor.matmul(
+                product[:],
+                weights[:, block * P : (block + 1) * P],
+                window[:].indirect(offsets[:]),
+                start=True,
+                stop=True,
+            )
+            staged = rows.tile([P, N + SENTENCES], F32, name="staged")
+            nc.vector.tensor_scalar_add(staged[:, 0:N], product[:], biases[block][:, 0:1])
+            sums = rows.tile([P, SENTENCES], F32, name="sums")
+            nc.vector.tensor_reduce(
+                sums[:],
+                staged[:, 0:N].rearrange("p (r t) -> p r t", t=LENGTH),
+                mybir.AxisListType.X,
+                mybir.AluOpType.add,
+            )
+            nc.vector.tensor_scalar_mul(staged[:, N : N + SENTENCES], sums[:], 1.0 / LENGTH)
+            queue = nc.sync if block == 0 else nc.scalar
+            queue.dma_start(out[block * P : (block + 1) * P, :], staged[:])

@@ -6,49 +6,49 @@ P = 128
 CHARS = 256
 N = 128
 SENTENCES, LENGTH = 4, 32
-BLOCKS = 2
+PAIR = 2
 
-FLOPS = 2 * P * BLOCKS * P * N
-BYTES = P * N * 2 + P * BLOCKS * P * 2 + BLOCKS * P * 4 + P * (N // 16) * 2 + BLOCKS * P * (N + SENTENCES) * 4
+FLOPS = 2 * P * PAIR * P * N
+BYTES = P * N * 2 + P * PAIR * P * 2 + PAIR * P * 4 + P * (N // 16) * 2 + PAIR * P * (N + SENTENCES) * 4
 
 
 def tile_ner_kernel(tc, table, w, b, offs, out):
     nc = tc.nc
     with (
         tc.tile_pool(name="held", bufs=1) as held,
-        tc.tile_pool(name="rows", bufs=BLOCKS) as rows,
-        tc.psum_pool(name="psum", bufs=BLOCKS) as psum,
+        tc.psum_pool(name="psum", bufs=PAIR) as psum,
     ):
         offsets = held.tile([P, N // 16], U16, name="offsets")
         nc.sync.dma_start(offsets[:], offs)
         window = held.tile([P, CHARS], BF16, name="window")
         nc.sync.dma_start(window[:], table)
-        weights = held.tile([P, BLOCKS * P], BF16, name="weights")
+        weights = held.tile([P, PAIR * P], BF16, name="weights")
         nc.scalar.dma_start(weights[:], w)
-        biases = []
-        for block in range(BLOCKS):
-            bias = held.tile([P, 1], F32, name=f"bias{block}")
-            nc.scalar.dma_start(bias[:], b[block * P : (block + 1) * P, :])
-            biases.append(bias)
+        bias = held.tile([P, PAIR], F32, name="bias")
+        nc.scalar.dma_start(bias[:], b.rearrange("(p half) one -> p (half one)", half=PAIR))
 
-        for block in range(BLOCKS):
+        columns_of = weights[:].rearrange("k (p half) -> k half p", half=PAIR)
+        staged = held.tile([P, PAIR, N + SENTENCES], F32, name="staged")
+        sums = held.tile([P, PAIR, SENTENCES], F32, name="sums")
+
+        for half in range(PAIR):
+            packed = held.tile([P, P], BF16, name=f"packed{half}")
+            nc.vector.tensor_copy(packed[:], columns_of[:, half, :])
             product = psum.tile([P, N], F32, name="product")
             nc.tensor.matmul(
                 product[:],
-                weights[:, block * P : (block + 1) * P],
+                packed[:],
                 window[:].indirect(offsets[:]),
                 start=True,
                 stop=True,
             )
-            staged = rows.tile([P, N + SENTENCES], F32, name="staged")
-            nc.vector.tensor_scalar_add(staged[:, 0:N], product[:], biases[block][:, 0:1])
-            sums = rows.tile([P, SENTENCES], F32, name="sums")
+            nc.vector.tensor_scalar_add(staged[:, half, 0:N], product[:], bias[:, half : half + 1])
             nc.vector.tensor_reduce(
-                sums[:],
-                staged[:, 0:N].rearrange("p (r t) -> p r t", t=LENGTH),
+                sums[:, half, :],
+                staged[:, half, 0:N].rearrange("p (r t) -> p r t", t=LENGTH),
                 mybir.AxisListType.X,
                 mybir.AluOpType.add,
             )
-            nc.vector.tensor_scalar_mul(staged[:, N : N + SENTENCES], sums[:], 1.0 / LENGTH)
-            queue = nc.sync if block == 0 else nc.scalar
-            queue.dma_start(out[block * P : (block + 1) * P, :], staged[:])
+            nc.vector.tensor_scalar_mul(staged[:, half, N : N + SENTENCES], sums[:, half, :], 1.0 / LENGTH)
+
+        nc.sync.dma_start(out.rearrange("(p half) c -> p half c", half=PAIR), staged[:])

@@ -42,13 +42,20 @@ def tile_ner_kernel(tc, table, w, b, offs, out):
                 start=True,
                 stop=True,
             )
-            nc.vector.tensor_scalar_add(staged[:, half, 0:N], product[:], bias[:, half : half + 1])
             nc.vector.tensor_reduce(
                 sums[:, half, :],
-                staged[:, half, 0:N].rearrange("p (r t) -> p r t", t=LENGTH),
+                product[:].rearrange("p (r t) -> p r t", t=LENGTH),
                 mybir.AxisListType.X,
                 mybir.AluOpType.add,
             )
-            nc.vector.tensor_scalar_mul(staged[:, half, N : N + SENTENCES], sums[:, half, :], 1.0 / LENGTH)
+            nc.vector.tensor_scalar_add(staged[:, half, 0:N], product[:], bias[:, half : half + 1])
+            nc.vector.tensor_scalar(
+                staged[:, half, N : N + SENTENCES],
+                sums[:, half, :],
+                1.0 / LENGTH,
+                bias[:, half : half + 1],
+                mybir.AluOpType.mult,
+                mybir.AluOpType.add,
+            )
 
         nc.sync.dma_start(out.rearrange("(p half) c -> p half c", half=PAIR), staged[:])

@@ -31,7 +31,7 @@ def tile_ner_kernel(tc, table, w, b, offs, out):
         staged = held.tile([P, PAIR, N + SENTENCES], F32, name="staged")
         sums = held.tile([P, PAIR, SENTENCES], F32, name="sums")
 
-        for half in range(PAIR):
+        def project(half):
             packed = held.tile([P, P], BF16, name=f"packed{half}")
             nc.vector.tensor_copy(packed[:], columns_of[:, half, :])
             product = psum.tile([P, N], F32, name="product")
@@ -58,4 +58,10 @@ def tile_ner_kernel(tc, table, w, b, offs, out):
                 mybir.AluOpType.add,
             )
 
-        nc.sync.dma_start(out.rearrange("(p half) c -> p half c", half=PAIR), staged[:])
+        staged_pairs = staged[:].rearrange("p half c -> p (half c)")
+        out_pairs = out.rearrange("(p half) c -> p (half c)", half=PAIR)
+
+        project(0)
+        nc.scalar.dma_start(out_pairs[:, 0:N], staged_pairs[:, 0:N])
+        project(1)
+        nc.sync.dma_start(out_pairs[:, N:], staged_pairs[:, N:])

@@ -6,62 +6,54 @@ P = 128
 CHARS = 256
 N = 128
 SENTENCES, LENGTH = 4, 32
-PAIR = 2
+BLOCKS = 2
 
-FLOPS = 2 * P * PAIR * P * N
-BYTES = P * N * 2 + P * PAIR * P * 2 + PAIR * P * 4 + P * (N // 16) * 2 + PAIR * P * (N + SENTENCES) * 4
+FLOPS = 2 * P * BLOCKS * P * N
+BYTES = P * N * 2 + P * BLOCKS * P * 2 + BLOCKS * P * 4 + P * (N // 16) * 2 + BLOCKS * P * (N + SENTENCES) * 4
 
 
 def tile_ner_kernel(tc, table, w, b, offs, out):
     nc = tc.nc
     with (
         tc.tile_pool(name="held", bufs=1) as held,
-        tc.psum_pool(name="psum", bufs=PAIR) as psum,
+        tc.psum_pool(name="psum", bufs=BLOCKS) as psum,
     ):
         offsets = held.tile([P, N // 16], U16, name="offsets")
         nc.sync.dma_start(offsets[:], offs)
         window = held.tile([P, CHARS], BF16, name="window")
         nc.sync.dma_start(window[:], table)
-        weights = held.tile([P, PAIR * P], BF16, name="weights")
+        weights = held.tile([P, BLOCKS * P], BF16, name="weights")
         nc.scalar.dma_start(weights[:], w)
-        bias = held.tile([P, PAIR], F32, name="bias")
-        nc.scalar.dma_start(bias[:], b.rearrange("(p half) one -> p (half one)", half=PAIR))
+        bias = held.tile([P, BLOCKS], F32, name="bias")
+        with nc.allow_non_contiguous_dma(reason="one float32 of the bias to a partition and block"):
+            nc.scalar.dma_start(bias[:], b.rearrange("(block p) one -> p (block one)", block=BLOCKS))
 
-        columns_of = weights[:].rearrange("k (p half) -> k half p", half=PAIR)
-        staged = held.tile([P, PAIR, N + SENTENCES], F32, name="staged")
-        sums = held.tile([P, PAIR, SENTENCES], F32, name="sums")
+        staged = held.tile([P, BLOCKS, N + SENTENCES], F32, name="staged")
+        sums = held.tile([P, BLOCKS, SENTENCES], F32, name="sums")
 
-        def project(half):
-            packed = held.tile([P, P], BF16, name=f"packed{half}")
-            nc.vector.tensor_copy(packed[:], columns_of[:, half, :])
+        for block in range(BLOCKS):
             product = psum.tile([P, N], F32, name="product")
             nc.tensor.matmul(
                 product[:],
-                packed[:],
+                weights[:, block * P : (block + 1) * P],
                 window[:].indirect(offsets[:]),
                 start=True,
                 stop=True,
             )
             nc.vector.tensor_reduce(
-                sums[:, half, :],
+                sums[:, block, :],
                 product[:].rearrange("p (r t) -> p r t", t=LENGTH),
                 mybir.AxisListType.X,
                 mybir.AluOpType.add,
             )
-            nc.vector.tensor_scalar_add(staged[:, half, 0:N], product[:], bias[:, half : half + 1])
+            nc.vector.tensor_scalar_add(staged[:, block, 0:N], product[:], bias[:, block : block + 1])
             nc.vector.tensor_scalar(
-                staged[:, half, N : N + SENTENCES],
-                sums[:, half, :],
+                staged[:, block, N : N + SENTENCES],
+                sums[:, block, :],
                 1.0 / LENGTH,
-                bias[:, half : half + 1],
+                bias[:, block : block + 1],
                 mybir.AluOpType.mult,
                 mybir.AluOpType.add,
             )
 
-        staged_pairs = staged[:].rearrange("p half c -> p (half c)")
-        out_pairs = out.rearrange("(p half) c -> p (half c)", half=PAIR)
-
-        project(0)
-        nc.scalar.dma_start(out_pairs[:, 0:N], staged_pairs[:, 0:N])
-        project(1)
-        nc.sync.dma_start(out_pairs[:, N:], staged_pairs[:, N:])
+        nc.sync.dma_start(out.rearrange("(block p) c -> p block c", block=BLOCKS), staged[:])

@@ -6,54 +6,56 @@ P = 128
 CHARS = 256
 N = 128
 SENTENCES, LENGTH = 4, 32
-BLOCKS = 2
+PAIR = 2
 
-FLOPS = 2 * P * BLOCKS * P * N
-BYTES = P * N * 2 + P * BLOCKS * P * 2 + BLOCKS * P * 4 + P * (N // 16) * 2 + BLOCKS * P * (N + SENTENCES) * 4
+FLOPS = 2 * P * PAIR * P * N
+BYTES = P * N * 2 + P * PAIR * P * 2 + PAIR * P * 4 + P * (N // 16) * 2 + PAIR * P * (N + SENTENCES) * 4
 
 
 def tile_ner_kernel(tc, table, w, b, offs, out):
     nc = tc.nc
     with (
         tc.tile_pool(name="held", bufs=1) as held,
-        tc.psum_pool(name="psum", bufs=BLOCKS) as psum,
+        tc.psum_pool(name="psum", bufs=PAIR) as psum,
     ):
+        weights = held.tile([P, PAIR * P], BF16, name="weights")
+        nc.sync.dma_start(weights[:], w)
         offsets = held.tile([P, N // 16], U16, name="offsets")
         nc.sync.dma_start(offsets[:], offs)
         window = held.tile([P, CHARS], BF16, name="window")
-        nc.sync.dma_start(window[:], table)
-        weights = held.tile([P, BLOCKS * P], BF16, name="weights")
-        nc.scalar.dma_start(weights[:], w)
-        bias = held.tile([P, BLOCKS], F32, name="bias")
-        with nc.allow_non_contiguous_dma(reason="one float32 of the bias to a partition and block"):
-            nc.scalar.dma_start(bias[:], b.rearrange("(block p) one -> p (block one)", block=BLOCKS))
+        nc.scalar.dma_start(window[:], table)
+        bias = held.tile([P, PAIR], F32, name="bias")
+        nc.scalar.dma_start(bias[:], b.rearrange("(p half) one -> p (half one)", half=PAIR))
 
-        staged = held.tile([P, BLOCKS, N + SENTENCES], F32, name="staged")
-        sums = held.tile([P, BLOCKS, SENTENCES], F32, name="sums")
+        columns_of = weights[:].rearrange("k (p half) -> k half p", half=PAIR)
+        staged = held.tile([P, PAIR, N + SENTENCES], F32, name="staged")
+        sums = held.tile([P, PAIR, SENTENCES], F32, name="sums")
 
-        for block in range(BLOCKS):
+        for half in range(PAIR):
+            packed = held.tile([P, P], BF16, name=f"packed{half}")
+            nc.vector.tensor_copy(packed[:], columns_of[:, half, :])
             product = psum.tile([P, N], F32, name="product")
             nc.tensor.matmul(
                 product[:],
-                weights[:, block * P : (block + 1) * P],
+                packed[:],
                 window[:].indirect(offsets[:]),
                 start=True,
                 stop=True,
             )
             nc.vector.tensor_reduce(
-                sums[:, block, :],
+                sums[:, half, :],
                 product[:].rearrange("p (r t) -> p r t", t=LENGTH),
                 mybir.AxisListType.X,
                 mybir.AluOpType.add,
             )
-            nc.vector.tensor_scalar_add(staged[:, block, 0:N], product[:], bias[:, block : block + 1])
+            nc.vector.tensor_scalar_add(staged[:, half, 0:N], product[:], bias[:, half : half + 1])
             nc.vector.tensor_scalar(
-                staged[:, block, N : N + SENTENCES],
-                sums[:, block, :],
+                staged[:, half, N : N + SENTENCES],
+                sums[:, half, :],
                 1.0 / LENGTH,
-                bias[:, block : block + 1],
+                bias[:, half : half + 1],
                 mybir.AluOpType.mult,
                 mybir.AluOpType.add,
             )
 
-        nc.sync.dma_start(out.rearrange("(block p) c -> p block c", block=BLOCKS), staged[:])
+        nc.sync.dma_start(out.rearrange("(p half) c -> p half c", half=PAIR), staged[:])

@@ -7,6 +7,7 @@ CHARS = 256
 N = 128
 SENTENCES, LENGTH = 4, 32
 PAIR = 2
+EDGE = 8
 
 FLOPS = 2 * P * PAIR * P * N
 BYTES = P * N * 2 + P * PAIR * P * 2 + PAIR * P * 4 + P * (N // 16) * 2 + PAIR * P * (N + SENTENCES) * 4
@@ -58,4 +59,8 @@ def tile_ner_kernel(tc, table, w, b, offs, out):
                 mybir.AluOpType.add,
             )
 
-        nc.sync.dma_start(out.rearrange("(p half) c -> p half c", half=PAIR), staged[:])
+        rows_in_hbm = out.rearrange("(p half) c -> p (half c)", half=PAIR)
+        rows_staged = staged[:].rearrange("p half c -> p (half c)")
+        cut = PAIR * (N + SENTENCES) - EDGE
+        nc.sync.dma_start(rows_in_hbm[:, 0:cut], rows_staged[:, 0:cut])
+        nc.scalar.dma_start(rows_in_hbm[:, cut:], rows_staged[:, cut:])

@@ -63,4 +63,4 @@ def tile_ner_kernel(tc, table, w, b, offs, out):
         rows_staged = staged[:].rearrange("p half c -> p (half c)")
         cut = PAIR * (N + SENTENCES) - EDGE
         nc.sync.dma_start(rows_in_hbm[:, 0:cut], rows_staged[:, 0:cut])
-        nc.scalar.dma_start(rows_in_hbm[:, cut:], rows_staged[:, cut:])
+        nc.sync.dma_start(rows_in_hbm[:, cut:], rows_staged[:, cut:])

@@ -13,6 +13,15 @@ FLOPS = 2 * P * PAIR * P * N
 BYTES = P * N * 2 + P * PAIR * P * 2 + PAIR * P * 4 + P * (N // 16) * 2 + PAIR * P * (N + SENTENCES) * 4
 
 
+def sum_sentences(nc, sums_of_half, product):
+    nc.vector.tensor_reduce(
+        sums_of_half,
+        product[:].rearrange("p (r t) -> p r t", t=LENGTH),
+        mybir.AxisListType.X,
+        mybir.AluOpType.add,
+    )
+
+
 def tile_ner_kernel(tc, table, w, b, offs, out):
     nc = tc.nc
     with (
@@ -43,13 +52,12 @@ def tile_ner_kernel(tc, table, w, b, offs, out):
                 start=True,
                 stop=True,
             )
-            nc.vector.tensor_reduce(
-                sums[:, half, :],
-                product[:].rearrange("p (r t) -> p r t", t=LENGTH),
-                mybir.AxisListType.X,
-                mybir.AluOpType.add,
-            )
-            nc.vector.tensor_scalar_add(staged[:, half, 0:N], product[:], bias[:, half : half + 1])
+            if half == 0:
+                sum_sentences(nc, sums[:, half, :], product)
+                nc.vector.tensor_scalar_add(staged[:, half, 0:N], product[:], bias[:, half : half + 1])
+            else:
+                nc.vector.tensor_scalar_add(staged[:, half, 0:N], product[:], bias[:, half : half + 1])
+                sum_sentences(nc, sums[:, half, :], product)
             nc.vector.tensor_scalar(
                 staged[:, half, N : N + SENTENCES],
                 sums[:, half, :],

@@ -22,6 +22,12 @@ def sum_sentences(nc, sums_of_half, product):
     )
 
 
+def add_bias(nc, characters, product, bias_of_half):
+    nc.vector.tensor_tensor(
+        characters, product[:], bias_of_half.to_broadcast([P, N]), mybir.AluOpType.add
+    )
+
+
 def tile_ner_kernel(tc, table, w, b, offs, out):
     nc = tc.nc
     with (
@@ -52,17 +58,18 @@ def tile_ner_kernel(tc, table, w, b, offs, out):
                 start=True,
                 stop=True,
             )
+            bias_of_half = bias[:, half : half + 1]
             if half == 0:
                 sum_sentences(nc, sums[:, half, :], product)
-                nc.vector.tensor_scalar_add(staged[:, half, 0:N], product[:], bias[:, half : half + 1])
+                add_bias(nc, staged[:, half, 0:N], product, bias_of_half)
             else:
-                nc.vector.tensor_scalar_add(staged[:, half, 0:N], product[:], bias[:, half : half + 1])
+                add_bias(nc, staged[:, half, 0:N], product, bias_of_half)
                 sum_sentences(nc, sums[:, half, :], product)
-            nc.vector.tensor_scalar(
+            nc.vector.scalar_tensor_tensor(
                 staged[:, half, N : N + SENTENCES],
                 sums[:, half, :],
                 1.0 / LENGTH,
-                bias[:, half : half + 1],
+                bias_of_half.to_broadcast([P, SENTENCES]),
                 mybir.AluOpType.mult,
                 mybir.AluOpType.add,
             )

import concourse.mybir as mybir

BF16, F32, U16 = mybir.dt.bfloat16, mybir.dt.float32, mybir.dt.uint16

P = 128
CHARS = 256
N = 128
SENTENCES, LENGTH = 4, 32
PAIR = 2
EDGE = 8

FLOPS = 2 * P * PAIR * P * N
BYTES = P * N * 2 + P * PAIR * P * 2 + PAIR * P * 4 + P * (N // 16) * 2 + PAIR * P * (N + SENTENCES) * 4


def sum_sentences(nc, sums_of_half, product):
    nc.vector.tensor_reduce(
        sums_of_half,
        product[:].rearrange("p (r t) -> p r t", t=LENGTH),
        mybir.AxisListType.X,
        mybir.AluOpType.add,
    )


def add_bias(nc, characters, product, bias_of_half):
    nc.vector.tensor_tensor(
        characters, product[:], bias_of_half.to_broadcast([P, N]), mybir.AluOpType.add
    )


def tile_ner_kernel(tc, table, w, b, offs, out):
    nc = tc.nc
    with (
        tc.tile_pool(name="held", bufs=1) as held,
        tc.psum_pool(name="psum", bufs=PAIR) as psum,
    ):
        weights = held.tile([P, PAIR * P], BF16, name="weights")
        nc.sync.dma_start(weights[:], w)
        offsets = held.tile([P, N // 16], U16, name="offsets")
        nc.sync.dma_start(offsets[:], offs)
        window = held.tile([P, CHARS], BF16, name="window")
        nc.scalar.dma_start(window[:], table)
        bias = held.tile([P, PAIR], F32, name="bias")
        nc.scalar.dma_start(bias[:], b.rearrange("(p half) one -> p (half one)", half=PAIR))

        columns_of = weights[:].rearrange("k (p half) -> k half p", half=PAIR)
        staged = held.tile([P, PAIR, N + SENTENCES], F32, name="staged")
        sums = held.tile([P, PAIR, SENTENCES], F32, name="sums")

        for half in range(PAIR):
            packed = held.tile([P, P], BF16, name=f"packed{half}")
            nc.vector.tensor_copy(packed[:], columns_of[:, half, :])
            product = psum.tile([P, N], F32, name="product")
            nc.tensor.matmul(
                product[:],
                packed[:],
                window[:].indirect(offsets[:]),
                start=True,
                stop=True,
            )
            bias_of_half = bias[:, half : half + 1]
            if half == 0:
                sum_sentences(nc, sums[:, half, :], product)
                add_bias(nc, staged[:, half, 0:N], product, bias_of_half)
            else:
                add_bias(nc, staged[:, half, 0:N], product, bias_of_half)
                sum_sentences(nc, sums[:, half, :], product)
            nc.vector.scalar_tensor_tensor(
                staged[:, half, N : N + SENTENCES],
                sums[:, half, :],
                1.0 / LENGTH,
                bias_of_half.to_broadcast([P, SENTENCES]),
                mybir.AluOpType.mult,
                mybir.AluOpType.add,
            )

        rows_in_hbm = out.rearrange("(p half) c -> p (half c)", half=PAIR)
        rows_staged = staged[:].rearrange("p half c -> p (half c)")
        cut = PAIR * (N + SENTENCES) - EDGE
        nc.sync.dma_start(rows_in_hbm[:, 0:cut], rows_staged[:, 0:cut])
        nc.sync.dma_start(rows_in_hbm[:, cut:], rows_staged[:, cut:])
